import numpy as np
import ml_dtypes


def mxq(x, axis, fmt="e4m3"):
    dtype, down = {"e4m3": (ml_dtypes.float8_e4m3fn, 7), "e5m2": (ml_dtypes.float8_e5m2, 14)}[fmt]
    v = np.moveaxis(np.asarray(x, np.float32).astype(ml_dtypes.bfloat16).astype(np.float64), axis, -1)
    blocks = v.reshape(v.shape[:-1] + (-1, 32))
    amax = np.abs(blocks).max(-1, keepdims=True)
    byte = np.maximum(np.where(amax > 0, np.frexp(amax)[1] - 1 + 127, 0) - down, 1)
    scale = np.exp2(byte - 127.0)
    codes = (blocks / scale).astype(np.float32).astype(dtype).astype(np.float64)
    return np.moveaxis((codes * scale).reshape(v.shape), -1, axis)


WIDE = False


def mx_kscale(k):
    if not WIDE:
        return np.ones(k)
    levels = np.array([10, -10, 5, -5, 0])
    a = np.random.permutation(np.resize(levels, k // 512 * 4)).reshape(k // 512, 4)
    idx = np.arange(k)
    return np.exp2(a[idx // 512, idx % 128 // 32])


BF16 = ml_dtypes.bfloat16


def bf(x):
    return np.asarray(x, np.float32).astype(BF16)


def f64(x):
    return np.asarray(x).astype(np.float64)


T, D, F, R = 512, 1024, 2560, 128


def setup_inputs():
    s = mx_kscale(F)
    return {
        "h": bf(np.random.standard_normal((T, F)) * 0.75 * s),
        "ha": bf(np.random.standard_normal((T, R)) * 0.75),
        "W_down": bf(np.random.standard_normal((F, D)) / np.sqrt(F) / s[:, None]),
        "B_down": bf(np.random.standard_normal((R, D)) * 0.5 / np.sqrt(R)),
    }


def reference(h, ha, W_down, B_down):
    return (mxq(f64(h), 1, "e4m3") @ mxq(f64(W_down), 0, "e4m3")) + f64(ha) @ f64(B_down)

@@ -1,0 +1,138 @@
+from contextlib import ExitStack
+
+import concourse.mybir as mybir
+from concourse.masks import make_identity
+
+F32 = mybir.dt.float32
+BF16 = mybir.dt.bfloat16
+U32 = mybir.dt.uint32
+U8 = mybir.dt.uint8
+FP8X4 = mybir.dt.float8_e4m3fn_x4
+ADD = mybir.AluOpType.add
+
+P = 128
+T, D, F, R = 512, 1024, 2560, 128
+K_PASS = 512
+G = F // K_PASS
+NT = T // P
+NC = D // 512
+
+FLOPS = 2 * T * F * D + 2 * T * R * D
+
+
+def tile_loramlp_pb_kernel(tc, h, ha, W_down, B_down, out):
+    nc = tc.nc
+    with ExitStack() as ctx:
+        keep = ctx.enter_context(tc.tile_pool(name="keep", bufs=1))
+        psum = ctx.enter_context(tc.psum_pool(name="psum", bufs=8))
+
+        ident_f = keep.tile([P, P], F32, name="ident_f")
+        make_identity(nc, ident_f[:])
+        ident_b = keep.tile([P, P], BF16, name="ident_b")
+        make_identity(nc, ident_b[:])
+
+        ha_sb = keep.tile([P, NT, R], BF16, name="ha_sb")
+        nc.sync.dma_start(out=ha_sb[:], in_=ha.rearrange("(i p) r -> p i r", p=P))
+        b_sb = keep.tile([P, D], BF16, name="b_sb")
+        nc.sync.dma_start(out=b_sb[:], in_=B_down)
+        h_raw = []
+        for i in range(NT):
+            t = keep.tile([P, F], BF16, name="h_raw%d" % i)
+            nc.sync.dma_start(out=t[:], in_=h[i * P : (i + 1) * P, :])
+            h_raw.append(t)
+        w_raw = []
+        for g in range(G):
+            t = keep.tile([P, 4 * D], BF16, name="w_raw%d" % g)
+            nc.sync.dma_start(
+                out=t[:].rearrange("p (u x) -> p u x", u=2),
+                in_=W_down[g * K_PASS : (g + 1) * K_PASS, :].rearrange("(u p e) c -> p u (e c)", u=2, p=P, e=2),
+            )
+            w_raw.append(t)
+
+        def evacuate(n, dst, src):
+            if n % 2 == 0:
+                nc.scalar.copy(out=dst, in_=src)
+            else:
+                nc.vector.tensor_copy(out=dst, in_=src)
+
+        haT_ps = psum.tile([P, NT, P], BF16, name="haT_ps", tag="bank")
+        for i in range(NT):
+            nc.tensor.transpose(haT_ps[:, i, :], ha_sb[:, i, :], ident_b[:])
+        haT = keep.tile([P, NT, P], BF16, name="haT")
+        nc.vector.tensor_copy(out=haT[:], in_=haT_ps[:])
+        lora = []
+        n = 0
+        for i in range(NT):
+            lo = keep.tile([P, D], F32, name="lora%d" % i)
+            lora.append(lo)
+            for c in range(NC):
+                ps = psum.tile([P, 512], F32, name="lora_ps", tag="bank")
+                nc.tensor.matmul(out=ps[:], lhsT=haT[:, i, :], rhs=b_sb[:, c * 512 : (c + 1) * 512], start=True, stop=True)
+                evacuate(n, lo[:, c * 512 : (c + 1) * 512], ps[:])
+                n += 1
+
+        hg_a = [keep.tile([P, 2048], BF16, name="hg_a%d" % i, align_bytes=64) for i in range(NT)]
+        hc_a = [keep.tile([P, 512], U32, name="hc_a%d" % i, align_bytes=64) for i in range(NT)]
+        hs_a = [keep.tile([P, 512], U8, name="hs_a%d" % i, align_bytes=64) for i in range(NT)]
+        hg_b = keep.tile([P, 2048], BF16, name="hg_b", align_bytes=64)
+        hc_b = keep.tile([P, 512], U32, name="hc_b", align_bytes=64)
+        hs_b = keep.tile([P, 512], U8, name="hs_b", align_bytes=64)
+
+        def words(i, g, u):
+            return h_raw[i][:].bitcast(F32)[:, 256 * g + 128 * u : 256 * g + 128 * u + 128]
+
+        n = 0
+        for i in range(NT):
+            dst32 = hg_a[i][:].bitcast(F32).rearrange("p (g r u) -> p g r u", g=4, r=P, u=2)
+            for g0 in (0, 2):
+                xt = psum.tile([P, 2, 2, P], F32, name="xt", tag="bank")
+                for gg in range(2):
+                    for u in range(2):
+                        nc.tensor.transpose(xt[:, gg, u, :], words(i, g0 + gg, u), ident_f[:])
+                evacuate(n, dst32[:, g0 : g0 + 2], xt[:].rearrange("p g u r -> p g r u"))
+                n += 1
+            if i % 2 == 1:
+                dst32 = hg_b[:].bitcast(F32).rearrange("p (i r u) -> p i r u", i=NT, r=P, u=2)
+                xt = psum.tile([P, 2, 2, P], F32, name="xt", tag="bank")
+                for ii in range(2):
+                    for u in range(2):
+                        nc.tensor.transpose(xt[:, ii, u, :], words(i - 1 + ii, 4, u), ident_f[:])
+                evacuate(n, dst32[:, i - 1 : i + 1], xt[:].rearrange("p g u r -> p g r u"))
+                n += 1
+            nc.vector.quantize_mx(out=hc_a[i][:].bitcast(FP8X4), scales=hs_a[i][:], in_=hg_a[i][:])
+        nc.vector.quantize_mx(out=hc_b[:].bitcast(FP8X4), scales=hs_b[:], in_=hg_b[:])
+
+        acc = [[psum.tile([P, 512], F32, name="acc%d%d" % (i, c), tag="bank") for c in range(NC)] for i in range(NT)]
+        for g in range(G):
+            src = w_raw[g][:].rearrange("p (t c) -> p t c", t=4)
+            for c in range(NC):
+                wg = keep.tile([P, 512, 4], BF16, name="wg%d%d" % (g, c), align_bytes=64)
+                wc = keep.tile([P, 512], U32, name="wc%d%d" % (g, c), align_bytes=64)
+                ws = keep.tile([P, 512], U8, name="ws%d%d" % (g, c), align_bytes=64)
+                d4 = wg[:].rearrange("p (c i) t -> p c t i", i=4)
+                s4 = src[:, :, c * 512 : (c + 1) * 512].rearrange("p t (c i) -> p c t i", i=4)
+                if c == 0:
+                    nc.vector.tensor_copy(out=d4, in_=s4)
+                else:
+                    nc.scalar.copy(out=d4, in_=s4)
+                nc.vector.quantize_mx(out=wc[:].bitcast(FP8X4), scales=ws[:], in_=wg[:].rearrange("p c t -> p (c t)"))
+                for i in range(NT):
+                    if g < 4:
+                        lhsT, lsc = hc_a[i][:, g * P : (g + 1) * P], hs_a[i][:, g * P : (g + 1) * P]
+                    else:
+                        lhsT, lsc = hc_b[:, i * P : (i + 1) * P], hs_b[:, i * P : (i + 1) * P]
+                    nc.tensor.matmul_mx(
+                        out=acc[i][c][:],
+                        lhsT=lhsT.bitcast(FP8X4),
+                        lhsT_scale=lsc,
+                        rhs=wc[:].bitcast(FP8X4),
+                        rhs_scale=ws[:],
+                        start=(g == 0),
+                        stop=(g == G - 1),
+                    )
+
+        for c in range(NC):
+            for i in range(NT):
+                cs = slice(c * 512, (c + 1) * 512)
+                nc.vector.tensor_tensor(out=lora[i][:, cs], in0=acc[i][c][:], in1=lora[i][:, cs], op=ADD)
+                nc.sync.dma_start(out=out[i * P : (i + 1) * P, cs], in_=lora[i][:, cs])

@@ -19,57 +19,86 @@ NC = D // 512
 
 FLOPS = 2 * T * F * D + 2 * T * R * D
 
+DMA_ORDER = ["ha","B","W0","h0","h1","h2","h3","W1","W2","W3","W4"]
+SPLIT_CHUNKS = []
+VCOLS = [[512,512],[256,256],[256,256],[256,256],[224,256]]
+LORA_ENG = ["V","S","V","S","V","S","V","S"]
+H_ENG = []
+W_ORDER = [[0,0],[0,1],[1,0],[1,1],[2,0],[2,1],[3,0],[3,1],[4,0],[4,1]]
+MANUAL = True
+PROGRAM = [["LH"],["L",0,0],["L",1,0],["L",2,0],["L",3,0],["L",0,1],["L",1,1],["L",2,1],["L",3,1],["WR",0,0],["WR",0,1],["WQ",0,0],["WQ",0,1],["HB",0,0,"S"],["HB",0,2,"S"],["HB",1,0,"S"],["HB",1,2,"S"],["HL",0,"S"],["HQ",0],["HQ",1],["HB",2,0,"S"],["HB",2,2,"S"],["HB",3,0,"S"],["HB",3,2,"S"],["HL",2,"S"],["HQ",2],["HQ",3],["HQL"],["P",0,0,0],["P",0,0,1],["P",0,0,2],["P",0,0,3],["P",0,1,0],["P",0,1,1],["P",0,1,2],["P",0,1,3],["WR",1,0],["WR",1,1],["WQ",1,0],["P",1,0,0],["P",1,0,1],["P",1,0,2],["P",1,0,3],["WQ",1,1],["P",1,1,0],["P",1,1,1],["P",1,1,2],["P",1,1,3],["WR",2,0],["WR",2,1],["WQ",2,0],["P",2,0,0],["P",2,0,1],["P",2,0,2],["P",2,0,3],["WQ",2,1],["P",2,1,0],["P",2,1,1],["P",2,1,2],["P",2,1,3],["WR",3,0],["WR",3,1],["WQ",3,0],["P",3,0,0],["P",3,0,1],["P",3,0,2],["P",3,0,3],["WQ",3,1],["P",3,1,0],["P",3,1,1],["P",3,1,2],["P",3,1,3],["WR",4,0],["WR",4,1],["WQ",4,0],["P",4,0,0],["P",4,0,1],["P",4,0,2],["P",4,0,3],["WQ",4,1],["P",4,1,0],["P",4,1,1],["P",4,1,2],["P",4,1,3],["F",0,0],["F",1,0],["F",2,0],["F",3,0],["F",0,1],["F",1,1],["F",2,1],["F",3,1]]
+
 
 def tile_loramlp_pb_kernel(tc, h, ha, W_down, B_down, out):
     nc = tc.nc
     with ExitStack() as ctx:
         keep = ctx.enter_context(tc.tile_pool(name="keep", bufs=1))
         psum = ctx.enter_context(tc.psum_pool(name="psum", bufs=8))
+        if MANUAL:
+            ctx.enter_context(tc.manual_schedule())
 
-        ident_f = keep.tile([P, P], F32, name="ident_f")
-        make_identity(nc, ident_f[:])
-        ident_b = keep.tile([P, P], BF16, name="ident_b")
-        make_identity(nc, ident_b[:])
+        h_v = h.rearrange("(p i) k -> p i k", i=NT)
+        out_v = out.rearrange("(p i) d -> p i d", i=NT)
 
         ha_sb = keep.tile([P, NT, R], BF16, name="ha_sb")
-        nc.sync.dma_start(out=ha_sb[:], in_=ha.rearrange("(i p) r -> p i r", p=P))
         b_sb = keep.tile([P, D], BF16, name="b_sb")
-        nc.sync.dma_start(out=b_sb[:], in_=B_down)
-        h_raw = []
-        for i in range(NT):
-            t = keep.tile([P, F], BF16, name="h_raw%d" % i)
-            nc.sync.dma_start(out=t[:], in_=h[i * P : (i + 1) * P, :])
-            h_raw.append(t)
-        w_raw = []
+        h_raw = [keep.tile([P, F], BF16, name="h_raw%d" % i) for i in range(NT)]
+        w_raw = {}
         for g in range(G):
-            t = keep.tile([P, 4 * D], BF16, name="w_raw%d" % g)
-            nc.sync.dma_start(
-                out=t[:].rearrange("p (u x) -> p u x", u=2),
-                in_=W_down[g * K_PASS : (g + 1) * K_PASS, :].rearrange("(u p e) c -> p u (e c)", u=2, p=P, e=2),
-            )
-            w_raw.append(t)
+            if g in SPLIT_CHUNKS:
+                for c in range(NC):
+                    w_raw[(g, c)] = keep.tile([P, 4, 512], BF16, name="w_raw%d%d" % (g, c))
+            else:
+                w_raw[(g, 0)] = keep.tile([P, 4, D], BF16, name="w_raw%d" % g)
 
-        def evacuate(n, dst, src):
-            if n % 2 == 0:
+        for what in DMA_ORDER:
+            if what == "ha":
+                nc.sync.dma_start(out=ha_sb[:], in_=ha.rearrange("(p i) r -> p i r", i=NT))
+            elif what == "B":
+                nc.sync.dma_start(out=b_sb[:], in_=B_down)
+            elif what[0] == "h":
+                i = int(what[1])
+                nc.sync.dma_start(out=h_raw[i][:], in_=h_v[:, i, :])
+            elif len(what) == 2:
+                g = int(what[1])
+                nc.sync.dma_start(
+                    out=w_raw[(g, 0)][:].rearrange("p (u e) c -> p u (e c)", u=2),
+                    in_=W_down[g * K_PASS : (g + 1) * K_PASS, :].rearrange("(u p e) c -> p u (e c)", u=2, p=P, e=2),
+                )
+            else:
+                g = int(what[1])
+                c = 0 if what[2] == "a" else 1
+                for u in range(2):
+                    r0 = g * K_PASS + u * 256
+                    nc.sync.dma_start(
+                        out=w_raw[(g, c)][:, 2 * u : 2 * u + 2, :],
+                        in_=W_down[r0 : r0 + 256, c * 512 : (c + 1) * 512].rearrange("(p e) c -> p e c", e=2),
+                    )
+
+        ident_b = keep.tile([P, P], BF16, name="ident_b")
+        make_identity(nc, ident_b[:])
+        ident_f = keep.tile([P, P], F32, name="ident_f")
+        make_identity(nc, ident_f[:])
+
+        def evacuate(eng, dst, src):
+            if eng == "S":
                 nc.scalar.copy(out=dst, in_=src)
             else:
                 nc.vector.tensor_copy(out=dst, in_=src)
 
-        haT_ps = psum.tile([P, NT, P], BF16, name="haT_ps", tag="bank")
-        for i in range(NT):
-            nc.tensor.transpose(haT_ps[:, i, :], ha_sb[:, i, :], ident_b[:])
+        lora = [keep.tile([P, D], F32, name="lora%d" % i) for i in range(NT)]
         haT = keep.tile([P, NT, P], BF16, name="haT")
-        nc.vector.tensor_copy(out=haT[:], in_=haT_ps[:])
-        lora = []
-        n = 0
-        for i in range(NT):
-            lo = keep.tile([P, D], F32, name="lora%d" % i)
-            lora.append(lo)
-            for c in range(NC):
-                ps = psum.tile([P, 512], F32, name="lora_ps", tag="bank")
-                nc.tensor.matmul(out=ps[:], lhsT=haT[:, i, :], rhs=b_sb[:, c * 512 : (c + 1) * 512], start=True, stop=True)
-                evacuate(n, lo[:, c * 512 : (c + 1) * 512], ps[:])
-                n += 1
+
+        def lora_head():
+            haT_ps = psum.tile([P, NT, P], BF16, name="haT_ps", tag="bank")
+            for i in range(NT):
+                nc.tensor.transpose(haT_ps[:, i, :], ha_sb[:, i, :], ident_b[:])
+            nc.vector.tensor_copy(out=haT[:], in_=haT_ps[:])
+
+        def lora_mm(i, c):
+            ps = psum.tile([P, 512], F32, name="lora_ps", tag="bank")
+            nc.tensor.matmul(out=ps[:], lhsT=haT[:, i, :], rhs=b_sb[:, c * 512 : (c + 1) * 512], start=True, stop=True)
+            evacuate(LORA_ENG[c * NT + i], lora[i][:, c * 512 : (c + 1) * 512], ps[:])
 
         hg_a = [keep.tile([P, 2048], BF16, name="hg_a%d" % i, align_bytes=64) for i in range(NT)]
         hc_a = [keep.tile([P, 512], U32, name="hc_a%d" % i, align_bytes=64) for i in range(NT)]
@@ -81,58 +110,103 @@ def tile_loramlp_pb_kernel(tc, h, ha, W_down, B_down, out):
         def words(i, g, u):
             return h_raw[i][:].bitcast(F32)[:, 256 * g + 128 * u : 256 * g + 128 * u + 128]
 
-        n = 0
-        for i in range(NT):
+        def h_bank(i, g0, eng):
             dst32 = hg_a[i][:].bitcast(F32).rearrange("p (g r u) -> p g r u", g=4, r=P, u=2)
-            for g0 in (0, 2):
-                xt = psum.tile([P, 2, 2, P], F32, name="xt", tag="bank")
-                for gg in range(2):
-                    for u in range(2):
-                        nc.tensor.transpose(xt[:, gg, u, :], words(i, g0 + gg, u), ident_f[:])
-                evacuate(n, dst32[:, g0 : g0 + 2], xt[:].rearrange("p g u r -> p g r u"))
-                n += 1
-            if i % 2 == 1:
-                dst32 = hg_b[:].bitcast(F32).rearrange("p (i r u) -> p i r u", i=NT, r=P, u=2)
-                xt = psum.tile([P, 2, 2, P], F32, name="xt", tag="bank")
-                for ii in range(2):
-                    for u in range(2):
-                        nc.tensor.transpose(xt[:, ii, u, :], words(i - 1 + ii, 4, u), ident_f[:])
-                evacuate(n, dst32[:, i - 1 : i + 1], xt[:].rearrange("p g u r -> p g r u"))
-                n += 1
+            xt = psum.tile([P, 2, 2, P], F32, name="xt", tag="bank")
+            for gg in range(2):
+                for u in range(2):
+                    nc.tensor.transpose(xt[:, gg, u, :], words(i, g0 + gg, u), ident_f[:])
+            evacuate(eng, dst32[:, g0 : g0 + 2], xt[:].rearrange("p g u r -> p g r u"))
+
+        def h_last(i0, eng):
+            dst32 = hg_b[:].bitcast(F32).rearrange("p (i r u) -> p i r u", i=NT, r=P, u=2)
+            xt = psum.tile([P, 2, 2, P], F32, name="xt", tag="bank")
+            for ii in range(2):
+                for u in range(2):
+                    nc.tensor.transpose(xt[:, ii, u, :], words(i0 + ii, 4, u), ident_f[:])
+            evacuate(eng, dst32[:, i0 : i0 + 2], xt[:].rearrange("p g u r -> p g r u"))
+
+        def h_quant(i):
             nc.vector.quantize_mx(out=hc_a[i][:].bitcast(FP8X4), scales=hs_a[i][:], in_=hg_a[i][:])
-        nc.vector.quantize_mx(out=hc_b[:].bitcast(FP8X4), scales=hs_b[:], in_=hg_b[:])
 
-        acc = [[psum.tile([P, 512], F32, name="acc%d%d" % (i, c), tag="bank") for c in range(NC)] for i in range(NT)]
-        for g in range(G):
-            src = w_raw[g][:].rearrange("p (t c) -> p t c", t=4)
-            for c in range(NC):
-                wg = keep.tile([P, 512, 4], BF16, name="wg%d%d" % (g, c), align_bytes=64)
-                wc = keep.tile([P, 512], U32, name="wc%d%d" % (g, c), align_bytes=64)
-                ws = keep.tile([P, 512], U8, name="ws%d%d" % (g, c), align_bytes=64)
-                d4 = wg[:].rearrange("p (c i) t -> p c t i", i=4)
-                s4 = src[:, :, c * 512 : (c + 1) * 512].rearrange("p t (c i) -> p c t i", i=4)
-                if c == 0:
-                    nc.vector.tensor_copy(out=d4, in_=s4)
-                else:
-                    nc.scalar.copy(out=d4, in_=s4)
-                nc.vector.quantize_mx(out=wc[:].bitcast(FP8X4), scales=ws[:], in_=wg[:].rearrange("p c t -> p (c t)"))
-                for i in range(NT):
-                    if g < 4:
-                        lhsT, lsc = hc_a[i][:, g * P : (g + 1) * P], hs_a[i][:, g * P : (g + 1) * P]
-                    else:
-                        lhsT, lsc = hc_b[:, i * P : (i + 1) * P], hs_b[:, i * P : (i + 1) * P]
-                    nc.tensor.matmul_mx(
-                        out=acc[i][c][:],
-                        lhsT=lhsT.bitcast(FP8X4),
-                        lhsT_scale=lsc,
-                        rhs=wc[:].bitcast(FP8X4),
-                        rhs_scale=ws[:],
-                        start=(g == 0),
-                        stop=(g == G - 1),
-                    )
+        def h_quant_last():
+            nc.vector.quantize_mx(out=hc_b[:].bitcast(FP8X4), scales=hs_b[:], in_=hg_b[:])
 
-        for c in range(NC):
-            for i in range(NT):
-                cs = slice(c * 512, (c + 1) * 512)
-                nc.vector.tensor_tensor(out=lora[i][:, cs], in0=acc[i][c][:], in1=lora[i][:, cs], op=ADD)
-                nc.sync.dma_start(out=out[i * P : (i + 1) * P, cs], in_=lora[i][:, cs])
+        wg = {}
+        wc = {}
+        ws = {}
+
+        def w_regroup(g, c):
+            wg[(g, c)] = keep.tile([P, 512, 4], BF16, name="wg%d%d" % (g, c), align_bytes=64)
+            if g in SPLIT_CHUNKS:
+                src = w_raw[(g, c)][:]
+            else:
+                src = w_raw[(g, 0)][:, :, c * 512 : (c + 1) * 512]
+            a = VCOLS[g][c]
+            if a > 0:
+                nc.vector.tensor_copy(
+                    out=wg[(g, c)][:, 0:a, :].rearrange("p (c i) t -> p c t i", i=4),
+                    in_=src[:, :, 0:a].rearrange("p t (c i) -> p c t i", i=4),
+                )
+            if a < 512:
+                nc.scalar.copy(
+                    out=wg[(g, c)][:, a:512, :].rearrange("p (c i) t -> p c t i", i=4),
+                    in_=src[:, :, a:512].rearrange("p t (c i) -> p c t i", i=4),
+                )
+
+        def w_quant(g, c):
+            wc[(g, c)] = keep.tile([P, 512], U32, name="wc%d%d" % (g, c), align_bytes=64)
+            ws[(g, c)] = keep.tile([P, 512], U8, name="ws%d%d" % (g, c), align_bytes=64)
+            nc.vector.quantize_mx(
+                out=wc[(g, c)][:].bitcast(FP8X4), scales=ws[(g, c)][:], in_=wg[(g, c)][:].rearrange("p c t -> p (c t)")
+            )
+
+        acc = {}
+        done = {}
+
+        def mx_pass(g, c, i):
+            if (i, c) not in acc:
+                acc[(i, c)] = psum.tile([P, 512], F32, name="acc%d%d" % (i, c), tag="bank")
+                done[(i, c)] = 0
+            if g < 4:
+                lhsT, lsc = hc_a[i][:, g * P : (g + 1) * P], hs_a[i][:, g * P : (g + 1) * P]
+            else:
+                lhsT, lsc = hc_b[:, i * P : (i + 1) * P], hs_b[:, i * P : (i + 1) * P]
+            nc.tensor.matmul_mx(
+                out=acc[(i, c)][:],
+                lhsT=lhsT.bitcast(FP8X4),
+                lhsT_scale=lsc,
+                rhs=wc[(g, c)][:].bitcast(FP8X4),
+                rhs_scale=ws[(g, c)][:],
+                start=(done[(i, c)] == 0),
+                stop=(done[(i, c)] == G - 1),
+            )
+            done[(i, c)] += 1
+
+        def finish(i, c):
+            cs = slice(c * 512, (c + 1) * 512)
+            nc.vector.tensor_tensor(out=lora[i][:, cs], in0=acc[(i, c)][:], in1=lora[i][:, cs], op=ADD)
+            nc.sync.dma_start(out=out_v[:, i, cs], in_=lora[i][:, cs])
+
+        for step in PROGRAM:
+            op = step[0]
+            if op == "LH":
+                lora_head()
+            elif op == "L":
+                lora_mm(step[1], step[2])
+            elif op == "HB":
+                h_bank(step[1], step[2], step[3])
+            elif op == "HL":
+                h_last(step[1], step[2])
+            elif op == "HQ":
+                h_quant(step[1])
+            elif op == "HQL":
+                h_quant_last()
+            elif op == "WR":
+                w_regroup(step[1], step[2])
+            elif op == "WQ":
+                w_quant(step[1], step[2])
+            elif op == "P":
+                mx_pass(step[1], step[2], step[3])
+            elif op == "F":
+                finish(step[1], step[2])

@@ -12,201 +12,157 @@ ADD = mybir.AluOpType.add
 
 P = 128
 T, D, F, R = 512, 1024, 2560, 128
-K_PASS = 512
-G = F // K_PASS
-NT = T // P
-NC = D // 512
+PACK = 4
+CHUNK = P * PACK
+CHUNKS = F // CHUNK
+TILES = T // P
+N = 512
+HALVES = D // N
+BANKS = 8
+
+VECTOR_COLS = 256
 
 FLOPS = 2 * T * F * D + 2 * T * R * D
-
-DMA_ORDER = ["ha","B","W0","h0","h1","h2","h3","W1","W2","W3","W4"]
-SPLIT_CHUNKS = []
-VCOLS = [[512,512],[256,256],[256,256],[256,256],[224,256]]
-LORA_ENG = ["V","S","V","S","V","S","V","S"]
-H_ENG = []
-W_ORDER = [[0,0],[0,1],[1,0],[1,1],[2,0],[2,1],[3,0],[3,1],[4,0],[4,1]]
-MANUAL = True
-PROGRAM = [["LH"],["L",0,0],["L",1,0],["L",2,0],["L",3,0],["L",0,1],["L",1,1],["L",2,1],["L",3,1],["WR",0,0],["WR",0,1],["WQ",0,0],["WQ",0,1],["HB",0,0,"S"],["HB",0,2,"S"],["HB",1,0,"S"],["HB",1,2,"S"],["HL",0,"S"],["HQ",0],["HQ",1],["HB",2,0,"S"],["HB",2,2,"S"],["HB",3,0,"S"],["HB",3,2,"S"],["HL",2,"S"],["HQ",2],["HQ",3],["HQL"],["P",0,0,0],["P",0,0,1],["P",0,0,2],["P",0,0,3],["P",0,1,0],["P",0,1,1],["P",0,1,2],["P",0,1,3],["WR",1,0],["WR",1,1],["WQ",1,0],["P",1,0,0],["P",1,0,1],["P",1,0,2],["P",1,0,3],["WQ",1,1],["P",1,1,0],["P",1,1,1],["P",1,1,2],["P",1,1,3],["WR",2,0],["WR",2,1],["WQ",2,0],["P",2,0,0],["P",2,0,1],["P",2,0,2],["P",2,0,3],["WQ",2,1],["P",2,1,0],["P",2,1,1],["P",2,1,2],["P",2,1,3],["WR",3,0],["WR",3,1],["WQ",3,0],["P",3,0,0],["P",3,0,1],["P",3,0,2],["P",3,0,3],["WQ",3,1],["P",3,1,0],["P",3,1,1],["P",3,1,2],["P",3,1,3],["WR",4,0],["WR",4,1],["WQ",4,0],["P",4,0,0],["P",4,0,1],["P",4,0,2],["P",4,0,3],["WQ",4,1],["P",4,1,0],["P",4,1,1],["P",4,1,2],["P",4,1,3],["F",0,0],["F",1,0],["F",2,0],["F",3,0],["F",0,1],["F",1,1],["F",2,1],["F",3,1]]
 
 
 def tile_loramlp_pb_kernel(tc, h, ha, W_down, B_down, out):
     nc = tc.nc
     with ExitStack() as ctx:
         keep = ctx.enter_context(tc.tile_pool(name="keep", bufs=1))
-        psum = ctx.enter_context(tc.psum_pool(name="psum", bufs=8))
-        if MANUAL:
-            ctx.enter_context(tc.manual_schedule())
+        psum = ctx.enter_context(tc.psum_pool(name="psum", bufs=BANKS))
+        ctx.enter_context(tc.manual_schedule())
 
-        h_v = h.rearrange("(p i) k -> p i k", i=NT)
-        out_v = out.rearrange("(p i) d -> p i d", i=NT)
+        h_tiles = h.rearrange("(p i) k -> p i k", i=TILES)
+        out_tiles = out.rearrange("(p i) d -> p i d", i=TILES)
 
-        ha_sb = keep.tile([P, NT, R], BF16, name="ha_sb")
+        ha_sb = keep.tile([P, TILES, R], BF16, name="ha_sb")
         b_sb = keep.tile([P, D], BF16, name="b_sb")
-        h_raw = [keep.tile([P, F], BF16, name="h_raw%d" % i) for i in range(NT)]
-        w_raw = {}
-        for g in range(G):
-            if g in SPLIT_CHUNKS:
-                for c in range(NC):
-                    w_raw[(g, c)] = keep.tile([P, 4, 512], BF16, name="w_raw%d%d" % (g, c))
-            else:
-                w_raw[(g, 0)] = keep.tile([P, 4, D], BF16, name="w_raw%d" % g)
+        h_raw = [keep.tile([P, F], BF16, name="h_raw%d" % i) for i in range(TILES)]
+        w_raw = [keep.tile([P, PACK, D], BF16, name="w_raw%d" % g) for g in range(CHUNKS)]
 
-        for what in DMA_ORDER:
-            if what == "ha":
-                nc.sync.dma_start(out=ha_sb[:], in_=ha.rearrange("(p i) r -> p i r", i=NT))
-            elif what == "B":
-                nc.sync.dma_start(out=b_sb[:], in_=B_down)
-            elif what[0] == "h":
-                i = int(what[1])
-                nc.sync.dma_start(out=h_raw[i][:], in_=h_v[:, i, :])
-            elif len(what) == 2:
-                g = int(what[1])
-                nc.sync.dma_start(
-                    out=w_raw[(g, 0)][:].rearrange("p (u e) c -> p u (e c)", u=2),
-                    in_=W_down[g * K_PASS : (g + 1) * K_PASS, :].rearrange("(u p e) c -> p u (e c)", u=2, p=P, e=2),
-                )
-            else:
-                g = int(what[1])
-                c = 0 if what[2] == "a" else 1
-                for u in range(2):
-                    r0 = g * K_PASS + u * 256
-                    nc.sync.dma_start(
-                        out=w_raw[(g, c)][:, 2 * u : 2 * u + 2, :],
-                        in_=W_down[r0 : r0 + 256, c * 512 : (c + 1) * 512].rearrange("(p e) c -> p e c", e=2),
-                    )
-
-        ident_b = keep.tile([P, P], BF16, name="ident_b")
-        make_identity(nc, ident_b[:])
-        ident_f = keep.tile([P, P], F32, name="ident_f")
-        make_identity(nc, ident_f[:])
-
-        def evacuate(eng, dst, src):
-            if eng == "S":
-                nc.scalar.copy(out=dst, in_=src)
-            else:
-                nc.vector.tensor_copy(out=dst, in_=src)
-
-        lora = [keep.tile([P, D], F32, name="lora%d" % i) for i in range(NT)]
-        haT = keep.tile([P, NT, P], BF16, name="haT")
-
-        def lora_head():
-            haT_ps = psum.tile([P, NT, P], BF16, name="haT_ps", tag="bank")
-            for i in range(NT):
-                nc.tensor.transpose(haT_ps[:, i, :], ha_sb[:, i, :], ident_b[:])
-            nc.vector.tensor_copy(out=haT[:], in_=haT_ps[:])
-
-        def lora_mm(i, c):
-            ps = psum.tile([P, 512], F32, name="lora_ps", tag="bank")
-            nc.tensor.matmul(out=ps[:], lhsT=haT[:, i, :], rhs=b_sb[:, c * 512 : (c + 1) * 512], start=True, stop=True)
-            evacuate(LORA_ENG[c * NT + i], lora[i][:, c * 512 : (c + 1) * 512], ps[:])
-
-        hg_a = [keep.tile([P, 2048], BF16, name="hg_a%d" % i, align_bytes=64) for i in range(NT)]
-        hc_a = [keep.tile([P, 512], U32, name="hc_a%d" % i, align_bytes=64) for i in range(NT)]
-        hs_a = [keep.tile([P, 512], U8, name="hs_a%d" % i, align_bytes=64) for i in range(NT)]
-        hg_b = keep.tile([P, 2048], BF16, name="hg_b", align_bytes=64)
-        hc_b = keep.tile([P, 512], U32, name="hc_b", align_bytes=64)
-        hs_b = keep.tile([P, 512], U8, name="hs_b", align_bytes=64)
-
-        def words(i, g, u):
-            return h_raw[i][:].bitcast(F32)[:, 256 * g + 128 * u : 256 * g + 128 * u + 128]
-
-        def h_bank(i, g0, eng):
-            dst32 = hg_a[i][:].bitcast(F32).rearrange("p (g r u) -> p g r u", g=4, r=P, u=2)
-            xt = psum.tile([P, 2, 2, P], F32, name="xt", tag="bank")
-            for gg in range(2):
-                for u in range(2):
-                    nc.tensor.transpose(xt[:, gg, u, :], words(i, g0 + gg, u), ident_f[:])
-            evacuate(eng, dst32[:, g0 : g0 + 2], xt[:].rearrange("p g u r -> p g r u"))
-
-        def h_last(i0, eng):
-            dst32 = hg_b[:].bitcast(F32).rearrange("p (i r u) -> p i r u", i=NT, r=P, u=2)
-            xt = psum.tile([P, 2, 2, P], F32, name="xt", tag="bank")
-            for ii in range(2):
-                for u in range(2):
-                    nc.tensor.transpose(xt[:, ii, u, :], words(i0 + ii, 4, u), ident_f[:])
-            evacuate(eng, dst32[:, i0 : i0 + 2], xt[:].rearrange("p g u r -> p g r u"))
-
-        def h_quant(i):
-            nc.vector.quantize_mx(out=hc_a[i][:].bitcast(FP8X4), scales=hs_a[i][:], in_=hg_a[i][:])
-
-        def h_quant_last():
-            nc.vector.quantize_mx(out=hc_b[:].bitcast(FP8X4), scales=hs_b[:], in_=hg_b[:])
-
-        wg = {}
-        wc = {}
-        ws = {}
-
-        def w_regroup(g, c):
-            wg[(g, c)] = keep.tile([P, 512, 4], BF16, name="wg%d%d" % (g, c), align_bytes=64)
-            if g in SPLIT_CHUNKS:
-                src = w_raw[(g, c)][:]
-            else:
-                src = w_raw[(g, 0)][:, :, c * 512 : (c + 1) * 512]
-            a = VCOLS[g][c]
-            if a > 0:
-                nc.vector.tensor_copy(
-                    out=wg[(g, c)][:, 0:a, :].rearrange("p (c i) t -> p c t i", i=4),
-                    in_=src[:, :, 0:a].rearrange("p t (c i) -> p c t i", i=4),
-                )
-            if a < 512:
-                nc.scalar.copy(
-                    out=wg[(g, c)][:, a:512, :].rearrange("p (c i) t -> p c t i", i=4),
-                    in_=src[:, :, a:512].rearrange("p t (c i) -> p c t i", i=4),
-                )
-
-        def w_quant(g, c):
-            wc[(g, c)] = keep.tile([P, 512], U32, name="wc%d%d" % (g, c), align_bytes=64)
-            ws[(g, c)] = keep.tile([P, 512], U8, name="ws%d%d" % (g, c), align_bytes=64)
-            nc.vector.quantize_mx(
-                out=wc[(g, c)][:].bitcast(FP8X4), scales=ws[(g, c)][:], in_=wg[(g, c)][:].rearrange("p c t -> p (c t)")
+        def load_w(g):
+            nc.sync.dma_start(
+                out=w_raw[g][:].rearrange("p (u e) c -> p u (e c)", u=2),
+                in_=W_down[g * CHUNK : (g + 1) * CHUNK, :].rearrange("(u p e) c -> p u (e c)", u=2, p=P, e=2),
             )
+
+        nc.sync.dma_start(out=ha_sb[:], in_=ha.rearrange("(p i) r -> p i r", i=TILES))
+        nc.sync.dma_start(out=b_sb[:], in_=B_down)
+        load_w(0)
+        for i in range(TILES):
+            nc.sync.dma_start(out=h_raw[i][:], in_=h_tiles[:, i, :])
+        for g in range(1, CHUNKS):
+            load_w(g)
+
+        ident_bf16 = keep.tile([P, P], BF16, name="ident_bf16")
+        make_identity(nc, ident_bf16[:])
+        ident_f32 = keep.tile([P, P], F32, name="ident_f32")
+        make_identity(nc, ident_f32[:])
+
+        result = [keep.tile([P, D], F32, name="result%d" % i) for i in range(TILES)]
+        haT_ps = psum.tile([P, TILES, P], BF16, name="haT_ps", tag="bank")
+        for i in range(TILES):
+            nc.tensor.transpose(haT_ps[:, i, :], ha_sb[:, i, :], ident_bf16[:])
+        haT = keep.tile([P, TILES, P], BF16, name="haT")
+        nc.vector.tensor_copy(out=haT[:], in_=haT_ps[:])
+        for c in range(HALVES):
+            cols = slice(c * N, (c + 1) * N)
+            for i in range(TILES):
+                lora_ps = psum.tile([P, N], F32, name="lora_ps", tag="bank")
+                nc.tensor.matmul(out=lora_ps[:], lhsT=haT[:, i, :], rhs=b_sb[:, cols], start=True, stop=True)
+                if i % 2 == 0:
+                    nc.vector.tensor_copy(out=result[i][:, cols], in_=lora_ps[:])
+                else:
+                    nc.scalar.copy(out=result[i][:, cols], in_=lora_ps[:])
+
+        w_grouped = {}
+        w_codes = {}
+        w_scales = {}
+
+        def regroup_w(g, c, vector_cols):
+            grouped = keep.tile([P, N, PACK], BF16, name="w_grouped%d%d" % (g, c), align_bytes=64)
+            w_grouped[(g, c)] = grouped
+            if vector_cols > 0:
+                nc.vector.tensor_copy(
+                    out=grouped[:, :vector_cols, :].rearrange("p (c i) t -> p c t i", i=4),
+                    in_=w_raw[g][:, :, c * N : c * N + vector_cols].rearrange("p t (c i) -> p c t i", i=4),
+                )
+            if vector_cols < N:
+                nc.scalar.copy(
+                    out=grouped[:, vector_cols:, :].rearrange("p (c i) t -> p c t i", i=4),
+                    in_=w_raw[g][:, :, c * N + vector_cols : (c + 1) * N].rearrange("p t (c i) -> p c t i", i=4),
+                )
+
+        def quantise_w(g, c):
+            w_codes[(g, c)] = keep.tile([P, N], U32, name="w_codes%d%d" % (g, c), align_bytes=64)
+            w_scales[(g, c)] = keep.tile([P, N], U8, name="w_scales%d%d" % (g, c), align_bytes=64)
+            nc.vector.quantize_mx(
+                out=w_codes[(g, c)][:].bitcast(FP8X4),
+                scales=w_scales[(g, c)][:],
+                in_=w_grouped[(g, c)][:].rearrange("p c t -> p (c t)"),
+            )
+
+        for c in range(HALVES):
+            regroup_w(0, c, N)
+        for c in range(HALVES):
+            quantise_w(0, c)
+
+        SETS = TILES + 1
+        h_grouped = [keep.tile([P, 4 * CHUNK], BF16, name="h_grouped%d" % s, align_bytes=64) for s in range(SETS)]
+        h_codes = [keep.tile([P, 4 * P], U32, name="h_codes%d" % s, align_bytes=64) for s in range(SETS)]
+        h_scales = [keep.tile([P, 4 * P], U8, name="h_scales%d" % s, align_bytes=64) for s in range(SETS)]
+
+        def transpose_two_blocks(s, first_block, sources):
+            bank = psum.tile([P, 2, 2, P], F32, name="h_ps", tag="bank")
+            for b, (i, g) in enumerate(sources):
+                for u in range(2):
+                    word = 256 * g + 128 * u
+                    nc.tensor.transpose(bank[:, b, u, :], h_raw[i][:].bitcast(F32)[:, word : word + P], ident_f32[:])
+            words = h_grouped[s][:].bitcast(F32).rearrange("p (b r u) -> p b r u", b=4, r=P, u=2)
+            nc.scalar.copy(out=words[:, first_block : first_block + 2], in_=bank[:].rearrange("p b u r -> p b r u"))
+
+        def quantise_h(s):
+            nc.vector.quantize_mx(out=h_codes[s][:].bitcast(FP8X4), scales=h_scales[s][:], in_=h_grouped[s][:])
+
+        for first_tile in range(0, TILES, 2):
+            pair = (first_tile, first_tile + 1)
+            for i in pair:
+                for g in (0, 2):
+                    transpose_two_blocks(i, g, [(i, g), (i, g + 1)])
+            transpose_two_blocks(TILES, first_tile, [(i, CHUNKS - 1) for i in pair])
+            for i in pair:
+                quantise_h(i)
+        quantise_h(TILES)
 
         acc = {}
-        done = {}
 
-        def mx_pass(g, c, i):
-            if (i, c) not in acc:
-                acc[(i, c)] = psum.tile([P, 512], F32, name="acc%d%d" % (i, c), tag="bank")
-                done[(i, c)] = 0
-            if g < 4:
-                lhsT, lsc = hc_a[i][:, g * P : (g + 1) * P], hs_a[i][:, g * P : (g + 1) * P]
-            else:
-                lhsT, lsc = hc_b[:, i * P : (i + 1) * P], hs_b[:, i * P : (i + 1) * P]
-            nc.tensor.matmul_mx(
-                out=acc[(i, c)][:],
-                lhsT=lhsT.bitcast(FP8X4),
-                lhsT_scale=lsc,
-                rhs=wc[(g, c)][:].bitcast(FP8X4),
-                rhs_scale=ws[(g, c)][:],
-                start=(done[(i, c)] == 0),
-                stop=(done[(i, c)] == G - 1),
-            )
-            done[(i, c)] += 1
+        def multiply(g, c):
+            for i in range(TILES):
+                if g == 0:
+                    acc[(i, c)] = psum.tile([P, N], F32, name="acc%d%d" % (i, c), tag="bank")
+                s, b = (i, g) if g < CHUNKS - 1 else (TILES, i)
+                block = slice(b * P, (b + 1) * P)
+                nc.tensor.matmul_mx(
+                    out=acc[(i, c)][:],
+                    lhsT=h_codes[s][:, block].bitcast(FP8X4),
+                    lhsT_scale=h_scales[s][:, block],
+                    rhs=w_codes[(g, c)][:].bitcast(FP8X4),
+                    rhs_scale=w_scales[(g, c)][:],
+                    start=(g == 0),
+                    stop=(g == CHUNKS - 1),
+                )
 
-        def finish(i, c):
-            cs = slice(c * 512, (c + 1) * 512)
-            nc.vector.tensor_tensor(out=lora[i][:, cs], in0=acc[(i, c)][:], in1=lora[i][:, cs], op=ADD)
-            nc.sync.dma_start(out=out_v[:, i, cs], in_=lora[i][:, cs])
+        for c in range(HALVES):
+            multiply(0, c)
+        for g in range(1, CHUNKS):
+            for c in range(HALVES):
+                regroup_w(g, c, VECTOR_COLS)
+            for c in range(HALVES):
+                quantise_w(g, c)
+                multiply(g, c)
 
-        for step in PROGRAM:
-            op = step[0]
-            if op == "LH":
-                lora_head()
-            elif op == "L":
-                lora_mm(step[1], step[2])
-            elif op == "HB":
-                h_bank(step[1], step[2], step[3])
-            elif op == "HL":
-                h_last(step[1], step[2])
-            elif op == "HQ":
-                h_quant(step[1])
-            elif op == "HQL":
-                h_quant_last()
-            elif op == "WR":
-                w_regroup(step[1], step[2])
-            elif op == "WQ":
-                w_quant(step[1], step[2])
-            elif op == "P":
-                mx_pass(step[1], step[2], step[3])
-            elif op == "F":
-                finish(step[1], step[2])
+        for c in range(HALVES):
+            cols = slice(c * N, (c + 1) * N)
+            for i in range(TILES):
+                nc.vector.tensor_tensor(out=result[i][:, cols], in0=acc[(i, c)][:], in1=result[i][:, cols], op=ADD)
+                nc.sync.dma_start(out=out_tiles[:, i, cols], in_=result[i][:, cols])

from contextlib import ExitStack

import concourse.mybir as mybir
from concourse.masks import make_identity

F32 = mybir.dt.float32
BF16 = mybir.dt.bfloat16
U32 = mybir.dt.uint32
U8 = mybir.dt.uint8
FP8X4 = mybir.dt.float8_e4m3fn_x4
ADD = mybir.AluOpType.add

P = 128
T, D, F, R = 512, 1024, 2560, 128
PACK = 4
CHUNK = P * PACK
CHUNKS = F // CHUNK
TILES = T // P
N = 512
HALVES = D // N
BANKS = 8

VECTOR_COLS = 256

FLOPS = 2 * T * F * D + 2 * T * R * D


def tile_loramlp_pb_kernel(tc, h, ha, W_down, B_down, out):
    nc = tc.nc
    with ExitStack() as ctx:
        keep = ctx.enter_context(tc.tile_pool(name="keep", bufs=1))
        psum = ctx.enter_context(tc.psum_pool(name="psum", bufs=BANKS))
        ctx.enter_context(tc.manual_schedule())

        h_tiles = h.rearrange("(p i) k -> p i k", i=TILES)
        out_tiles = out.rearrange("(p i) d -> p i d", i=TILES)

        ha_sb = keep.tile([P, TILES, R], BF16, name="ha_sb")
        b_sb = keep.tile([P, D], BF16, name="b_sb")
        h_raw = [keep.tile([P, F], BF16, name="h_raw%d" % i) for i in range(TILES)]
        w_raw = [keep.tile([P, PACK, D], BF16, name="w_raw%d" % g) for g in range(CHUNKS)]

        def load_w(g):
            nc.sync.dma_start(
                out=w_raw[g][:].rearrange("p (u e) c -> p u (e c)", u=2),
                in_=W_down[g * CHUNK : (g + 1) * CHUNK, :].rearrange("(u p e) c -> p u (e c)", u=2, p=P, e=2),
            )

        nc.sync.dma_start(out=ha_sb[:], in_=ha.rearrange("(p i) r -> p i r", i=TILES))
        nc.sync.dma_start(out=b_sb[:], in_=B_down)
        load_w(0)
        for i in range(TILES):
            nc.sync.dma_start(out=h_raw[i][:], in_=h_tiles[:, i, :])
        for g in range(1, CHUNKS):
            load_w(g)

        ident_bf16 = keep.tile([P, P], BF16, name="ident_bf16")
        make_identity(nc, ident_bf16[:])
        ident_f32 = keep.tile([P, P], F32, name="ident_f32")
        make_identity(nc, ident_f32[:])

        result = [keep.tile([P, D], F32, name="result%d" % i) for i in range(TILES)]
        haT_ps = psum.tile([P, TILES, P], BF16, name="haT_ps", tag="bank")
        for i in range(TILES):
            nc.tensor.transpose(haT_ps[:, i, :], ha_sb[:, i, :], ident_bf16[:])
        haT = keep.tile([P, TILES, P], BF16, name="haT")
        nc.vector.tensor_copy(out=haT[:], in_=haT_ps[:])
        for c in range(HALVES):
            cols = slice(c * N, (c + 1) * N)
            for i in range(TILES):
                lora_ps = psum.tile([P, N], F32, name="lora_ps", tag="bank")
                nc.tensor.matmul(out=lora_ps[:], lhsT=haT[:, i, :], rhs=b_sb[:, cols], start=True, stop=True)
                if i % 2 == 0:
                    nc.vector.tensor_copy(out=result[i][:, cols], in_=lora_ps[:])
                else:
                    nc.scalar.copy(out=result[i][:, cols], in_=lora_ps[:])

        w_grouped = {}
        w_codes = {}
        w_scales = {}

        def regroup_w(g, c, vector_cols):
            grouped = keep.tile([P, N, PACK], BF16, name="w_grouped%d%d" % (g, c), align_bytes=64)
            w_grouped[(g, c)] = grouped
            if vector_cols > 0:
                nc.vector.tensor_copy(
                    out=grouped[:, :vector_cols, :].rearrange("p (c i) t -> p c t i", i=4),
                    in_=w_raw[g][:, :, c * N : c * N + vector_cols].rearrange("p t (c i) -> p c t i", i=4),
                )
            if vector_cols < N:
                nc.scalar.copy(
                    out=grouped[:, vector_cols:, :].rearrange("p (c i) t -> p c t i", i=4),
                    in_=w_raw[g][:, :, c * N + vector_cols : (c + 1) * N].rearrange("p t (c i) -> p c t i", i=4),
                )

        def quantise_w(g, c):
            w_codes[(g, c)] = keep.tile([P, N], U32, name="w_codes%d%d" % (g, c), align_bytes=64)
            w_scales[(g, c)] = keep.tile([P, N], U8, name="w_scales%d%d" % (g, c), align_bytes=64)
            nc.vector.quantize_mx(
                out=w_codes[(g, c)][:].bitcast(FP8X4),
                scales=w_scales[(g, c)][:],
                in_=w_grouped[(g, c)][:].rearrange("p c t -> p (c t)"),
            )

        for c in range(HALVES):
            regroup_w(0, c, N)
        for c in range(HALVES):
            quantise_w(0, c)

        SETS = TILES + 1
        h_grouped = [keep.tile([P, 4 * CHUNK], BF16, name="h_grouped%d" % s, align_bytes=64) for s in range(SETS)]
        h_codes = [keep.tile([P, 4 * P], U32, name="h_codes%d" % s, align_bytes=64) for s in range(SETS)]
        h_scales = [keep.tile([P, 4 * P], U8, name="h_scales%d" % s, align_bytes=64) for s in range(SETS)]

        def transpose_two_blocks(s, first_block, sources):
            bank = psum.tile([P, 2, 2, P], F32, name="h_ps", tag="bank")
            for b, (i, g) in enumerate(sources):
                for u in range(2):
                    word = 256 * g + 128 * u
                    nc.tensor.transpose(bank[:, b, u, :], h_raw[i][:].bitcast(F32)[:, word : word + P], ident_f32[:])
            words = h_grouped[s][:].bitcast(F32).rearrange("p (b r u) -> p b r u", b=4, r=P, u=2)
            nc.scalar.copy(out=words[:, first_block : first_block + 2], in_=bank[:].rearrange("p b u r -> p b r u"))

        def quantise_h(s):
            nc.vector.quantize_mx(out=h_codes[s][:].bitcast(FP8X4), scales=h_scales[s][:], in_=h_grouped[s][:])

        for first_tile in range(0, TILES, 2):
            pair = (first_tile, first_tile + 1)
            for i in pair:
                for g in (0, 2):
                    transpose_two_blocks(i, g, [(i, g), (i, g + 1)])
            transpose_two_blocks(TILES, first_tile, [(i, CHUNKS - 1) for i in pair])
            for i in pair:
                quantise_h(i)
        quantise_h(TILES)

        acc = {}

        def multiply(g, c):
            for i in range(TILES):
                if g == 0:
                    acc[(i, c)] = psum.tile([P, N], F32, name="acc%d%d" % (i, c), tag="bank")
                s, b = (i, g) if g < CHUNKS - 1 else (TILES, i)
                block = slice(b * P, (b + 1) * P)
                nc.tensor.matmul_mx(
                    out=acc[(i, c)][:],
                    lhsT=h_codes[s][:, block].bitcast(FP8X4),
                    lhsT_scale=h_scales[s][:, block],
                    rhs=w_codes[(g, c)][:].bitcast(FP8X4),
                    rhs_scale=w_scales[(g, c)][:],
                    start=(g == 0),
                    stop=(g == CHUNKS - 1),
                )

        for c in range(HALVES):
            multiply(0, c)
        for g in range(1, CHUNKS):
            for c in range(HALVES):
                regroup_w(g, c, VECTOR_COLS)
            for c in range(HALVES):
                quantise_w(g, c)
                multiply(g, c)

        for c in range(HALVES):
            cols = slice(c * N, (c + 1) * N)
            for i in range(TILES):
                nc.vector.tensor_tensor(out=result[i][:, cols], in0=acc[(i, c)][:], in1=result[i][:, cols], op=ADD)
                nc.sync.dma_start(out=out_tiles[:, i, cols], in_=result[i][:, cols])
